import numpy as np
import ml_dtypes


def mxq(x, axis, fmt="e4m3"):
    dtype, down = {"e4m3": (ml_dtypes.float8_e4m3fn, 7), "e5m2": (ml_dtypes.float8_e5m2, 14)}[fmt]
    v = np.moveaxis(np.asarray(x, np.float32).astype(ml_dtypes.bfloat16).astype(np.float64), axis, -1)
    blocks = v.reshape(v.shape[:-1] + (-1, 32))
    amax = np.abs(blocks).max(-1, keepdims=True)
    byte = np.maximum(np.where(amax > 0, np.frexp(amax)[1] - 1 + 127, 0) - down, 1)
    scale = np.exp2(byte - 127.0)
    codes = (blocks / scale).astype(np.float32).astype(dtype).astype(np.float64)
    return np.moveaxis((codes * scale).reshape(v.shape), -1, axis)


BF16 = ml_dtypes.bfloat16


def bf(x):
    return np.asarray(x, np.float32).astype(BF16)


def f64(x):
    return np.asarray(x).astype(np.float64)


B, L, D = 16, 1024, 256

EPS = 1e-05


def setup_inputs():
    g = 0.5 + np.random.random_sample((B, L, 1))
    c = 1.8 / (L * np.sqrt(D)) ** (1.0 / 3.0)
    return {"inputs": bf(np.random.standard_normal((B, L, D)) * g * c)}


def reference(inputs):
    x = f64(inputs)
    w = np.sqrt(EPS + np.sum(x * x, axis=-1))
    xw = x * w[..., None]
    return mxq(xw, 1, "e4m3").transpose(0, 2, 1) @ mxq(x, 1, "e4m3")

@@ -1,0 +1,145 @@
+from contextlib import ExitStack
+
+import concourse.mybir as mybir
+
+FLOPS = 2 * 16 * 1024 * 256 * 256
+
+BF16 = mybir.dt.bfloat16
+F32 = mybir.dt.float32
+U32 = mybir.dt.uint32
+U8 = mybir.dt.uint8
+FP8X4 = mybir.dt.float8_e4m3fn_x4
+ACT = mybir.ActivationFunctionType
+ALU = mybir.AluOpType
+
+P = 128
+B = 16
+L = 1024
+D = 256
+PACK = 4
+PASSES = L // (P * PACK)
+SLOTS = PASSES * PACK
+EPS = 1e-05
+
+
+def tile_globalmixture_t_kernel(tc, inputs, out):
+    nc = tc.nc
+    x_view = inputs.rearrange("b (c p t) d -> p b c (t d)", c=PASSES, p=P, t=PACK)
+    o_view = out.rearrange("b (m p) e -> p b m e", m=2, p=P)
+
+    with ExitStack() as ctx:
+        ctx.enter_context(tc.manual_schedule())
+        keep = ctx.enter_context(tc.tile_pool(name="keep", bufs=1))
+        junkp = ctx.enter_context(tc.tile_pool(name="junkp", bufs=4))
+        small = ctx.enter_context(tc.tile_pool(name="small", bufs=4))
+        natp = ctx.enter_context(tc.tile_pool(name="natp", bufs=2))
+        grp = ctx.enter_context(tc.tile_pool(name="grp", bufs=3))
+        codes = ctx.enter_context(tc.tile_pool(name="codes", bufs=3))
+        outp = ctx.enter_context(tc.tile_pool(name="outp", bufs=4))
+        psum = ctx.enter_context(tc.psum_pool(name="psum", bufs=4))
+
+        eps = keep.tile([P, 1], F32, name="eps")
+        nc.vector.memset(eps[:], EPS)
+        warm = keep.tile([P, 1], F32, name="warm")
+        nc.scalar.activation(out=warm[:], in_=eps[:], func=ACT.Sqrt)
+
+        xs = []
+        for b in range(B):
+            x_b = keep.tile([P, SLOTS, D], BF16, name="x%d" % b)
+            nc.sync.dma_start(
+                out=x_b[:].rearrange("p (c t) d -> p c (t d)", c=PASSES),
+                in_=x_view[:, b],
+            )
+            xs.append(x_b)
+
+        sums = {}
+        norms = {}
+        gxs = {}
+        cxs = {}
+
+        def sum_squares(b):
+            ss = small.tile([P, SLOTS], F32, name="ss")
+            for s in range(SLOTS):
+                junk = junkp.tile([P, D], BF16, name="junk")
+                nc.scalar.activation(
+                    out=junk[:],
+                    in_=xs[b][:, s, :],
+                    func=ACT.Square,
+                    accum_out=ss[:, s : s + 1],
+                )
+            sums[b] = ss
+
+        def norm(b):
+            w = small.tile([P, SLOTS], F32, name="w")
+            nc.scalar.activation(out=w[:], in_=sums[b][:], func=ACT.Sqrt, bias=eps[:])
+            norms[b] = w
+
+        def regroup(dst, src):
+            nc.vector.tensor_copy(
+                out=dst[:].rearrange("p g (c i) t -> p g c t i", i=4),
+                in_=src[:].rearrange("p (g t) (c i) -> p g c t i", g=PASSES, i=4),
+            )
+
+        def regroup_x(b):
+            gx = grp.tile([P, PASSES, D, PACK], BF16, name="gx", align_bytes=64)
+            regroup(gx, xs[b])
+            gxs[b] = gx
+
+        def quantise(g, tag):
+            c = codes.tile([P, PASSES * D], U32, name="c" + tag, align_bytes=64)
+            s = codes.tile([P, PASSES * D], U8, name="s" + tag, align_bytes=64)
+            nc.vector.quantize_mx(
+                out=c[:].bitcast(FP8X4),
+                scales=s[:],
+                in_=g[:].rearrange("p g d t -> p (g d t)"),
+            )
+            return c, s
+
+        sum_squares(0)
+        norm(0)
+        sum_squares(1)
+        norm(1)
+        regroup_x(0)
+        regroup_x(1)
+        cxs[0] = quantise(gxs[0], "x")
+
+        for b in range(B):
+            if b + 2 < B:
+                sum_squares(b + 2)
+                norm(b + 2)
+            xw = natp.tile([P, SLOTS, D], BF16, name="xw")
+            for s in range(SLOTS):
+                nc.vector.tensor_scalar(
+                    out=xw[:, s, :],
+                    in0=xs[b][:, s, :],
+                    scalar1=norms[b][:, s : s + 1],
+                    scalar2=None,
+                    op0=ALU.mult,
+                )
+            if b + 1 < B:
+                cxs[b + 1] = quantise(gxs[b + 1], "x")
+            gw = grp.tile([P, PASSES, D, PACK], BF16, name="gw", align_bytes=64)
+            regroup(gw, xw)
+            if b + 2 < B:
+                regroup_x(b + 2)
+            cw, sw = quantise(gw, "w")
+            cx, sx = cxs[b]
+
+            ps = psum.tile([P, 2 * D], F32, name="ps")
+            for m in range(2):
+                for c in range(PASSES):
+                    lo = c * D + m * P
+                    nc.tensor.matmul_mx(
+                        out=ps[:, m * D : (m + 1) * D],
+                        lhsT=cw[:, lo : lo + P].bitcast(FP8X4),
+                        lhsT_scale=sw[:, lo : lo + P],
+                        rhs=cx[:, c * D : (c + 1) * D].bitcast(FP8X4),
+                        rhs_scale=sx[:, c * D : (c + 1) * D],
+                        start=(c == 0),
+                        stop=(c == PASSES - 1),
+                    )
+            o_b = outp.tile([P, 2 * D], F32, name="o_b")
+            nc.scalar.copy(out=o_b[:], in_=ps[:])
+            nc.sync.dma_start(
+                out=o_view[:, b], in_=o_b[:].rearrange("p (m e) -> p m e", m=2)
+            )

@@ -20,6 +20,7 @@ PACK = 4
 PASSES = L // (P * PACK)
 SLOTS = PASSES * PACK
 EPS = 1e-05
+SHARE = 104
 
 
 def tile_globalmixture_t_kernel(tc, inputs, out):
@@ -33,10 +34,11 @@ def tile_globalmixture_t_kernel(tc, inputs, out):
         junkp = ctx.enter_context(tc.tile_pool(name="junkp", bufs=4))
         small = ctx.enter_context(tc.tile_pool(name="small", bufs=4))
         natp = ctx.enter_context(tc.tile_pool(name="natp", bufs=2))
-        grp = ctx.enter_context(tc.tile_pool(name="grp", bufs=3))
+        grp = ctx.enter_context(tc.tile_pool(name="grp", bufs=4))
         codes = ctx.enter_context(tc.tile_pool(name="codes", bufs=3))
         outp = ctx.enter_context(tc.tile_pool(name="outp", bufs=4))
         psum = ctx.enter_context(tc.psum_pool(name="psum", bufs=4))
+        psum1 = ctx.enter_context(tc.psum_pool(name="psum1", bufs=1))
 
         eps = keep.tile([P, 1], F32, name="eps")
         nc.vector.memset(eps[:], EPS)
@@ -46,16 +48,20 @@ def tile_globalmixture_t_kernel(tc, inputs, out):
         xs = []
         for b in range(B):
             x_b = keep.tile([P, SLOTS, D], BF16, name="x%d" % b)
-            nc.sync.dma_start(
-                out=x_b[:].rearrange("p (c t) d -> p c (t d)", c=PASSES),
-                in_=x_view[:, b],
-            )
+            x_rows = x_b[:].rearrange("p (c t) d -> p c (t d)", c=PASSES)
+            if b == 0:
+                for c in range(PASSES):
+                    nc.sync.dma_start(out=x_rows[:, c, :], in_=x_view[:, b, c, :])
+            else:
+                nc.sync.dma_start(out=x_rows, in_=x_view[:, b])
             xs.append(x_b)
 
         sums = {}
         norms = {}
         gxs = {}
         cxs = {}
+        xws = {}
+        pss = {}
 
         def sum_squares(b):
             ss = small.tile([P, SLOTS], F32, name="ss")
@@ -74,20 +80,53 @@ def tile_globalmixture_t_kernel(tc, inputs, out):
             nc.scalar.activation(out=w[:], in_=sums[b][:], func=ACT.Sqrt, bias=eps[:])
             norms[b] = w
 
-        def regroup(dst, src):
-            nc.vector.tensor_copy(
-                out=dst[:].rearrange("p g (c i) t -> p g c t i", i=4),
-                in_=src[:].rearrange("p (g t) (c i) -> p g c t i", g=PASSES, i=4),
+        def regroup_pass(copy, dst, src):
+            copy(
+                out=dst.rearrange("p (c i) t -> p c t i", i=4),
+                in_=src.rearrange("p t (c i) -> p c t i", i=4),
             )
 
-        def regroup_x(b):
+        def regroup_both(dst, src):
+            nc.vector.tensor_copy(
+                out=dst.rearrange("p g (c i) t -> p g c t i", i=4),
+                in_=src.rearrange("p (g t) (c i) -> p g c t i", t=PACK, i=4),
+            )
+
+        def new_gx(b):
             gx = grp.tile([P, PASSES, D, PACK], BF16, name="gx", align_bytes=64)
-            regroup(gx, xs[b])
             gxs[b] = gx
 
-        def quantise(g, tag):
-            c = codes.tile([P, PASSES * D], U32, name="c" + tag, align_bytes=64)
-            s = codes.tile([P, PASSES * D], U8, name="s" + tag, align_bytes=64)
+        def scalar_regroup_x(b):
+            new_gx(b)
+            regroup_pass(
+                nc.scalar.copy,
+                gxs[b][:, 1, D - SHARE :, :],
+                xs[b][:, PACK:, D - SHARE :],
+            )
+
+        def vector_regroup_x(b):
+            if b in gxs:
+                regroup_pass(nc.vector.tensor_copy, gxs[b][:, 0, :, :], xs[b][:, :PACK, :])
+                regroup_pass(
+                    nc.vector.tensor_copy,
+                    gxs[b][:, 1, : D - SHARE, :],
+                    xs[b][:, PACK:, : D - SHARE],
+                )
+            else:
+                new_gx(b)
+                if b == 0:
+                    for c in range(PASSES):
+                        regroup_pass(
+                            nc.vector.tensor_copy,
+                            gxs[b][:, c, :, :],
+                            xs[b][:, c * PACK : (c + 1) * PACK, :],
+                        )
+                else:
+                    regroup_both(gxs[b][:], xs[b][:])
+
+        def quantise(g, width, tag, pool):
+            c = pool.tile([P, width // PACK], U32, name="c" + tag, align_bytes=64)
+            s = pool.tile([P, width // PACK], U8, name="s" + tag, align_bytes=64)
             nc.vector.quantize_mx(
                 out=c[:].bitcast(FP8X4),
                 scales=s[:],
@@ -95,18 +134,10 @@ def tile_globalmixture_t_kernel(tc, inputs, out):
             )
             return c, s
 
-        sum_squares(0)
-        norm(0)
-        sum_squares(1)
-        norm(1)
-        regroup_x(0)
-        regroup_x(1)
-        cxs[0] = quantise(gxs[0], "x")
+        def quantise_x(b):
+            cxs[b] = quantise(gxs[b], PASSES * D * PACK, "x", codes)
 
-        for b in range(B):
-            if b + 2 < B:
-                sum_squares(b + 2)
-                norm(b + 2)
+        def scale(b):
             xw = natp.tile([P, SLOTS, D], BF16, name="xw")
             for s in range(SLOTS):
                 nc.vector.tensor_scalar(
@@ -116,30 +147,90 @@ def tile_globalmixture_t_kernel(tc, inputs, out):
                     scalar2=None,
                     op0=ALU.mult,
                 )
-            if b + 1 < B:
-                cxs[b + 1] = quantise(gxs[b + 1], "x")
-            gw = grp.tile([P, PASSES, D, PACK], BF16, name="gw", align_bytes=64)
-            regroup(gw, xw)
-            if b + 2 < B:
-                regroup_x(b + 2)
-            cw, sw = quantise(gw, "w")
-            cx, sx = cxs[b]
+            xws[b] = xw
 
+        def group(acc, cw, sw, stride, lo, b):
+            cx, sx = cxs[b]
+            for c in range(PASSES):
+                nc.tensor.matmul_mx(
+                    out=acc,
+                    lhsT=cw[:, c * stride + lo : c * stride + lo + P].bitcast(FP8X4),
+                    lhsT_scale=sw[:, c * stride + lo : c * stride + lo + P],
+                    rhs=cx[:, c * D : (c + 1) * D].bitcast(FP8X4),
+                    rhs_scale=sx[:, c * D : (c + 1) * D],
+                    start=(c == 0),
+                    stop=(c == PASSES - 1),
+                )
+
+        def multiply(b, cw, sw):
             ps = psum.tile([P, 2 * D], F32, name="ps")
             for m in range(2):
-                for c in range(PASSES):
-                    lo = c * D + m * P
-                    nc.tensor.matmul_mx(
-                        out=ps[:, m * D : (m + 1) * D],
-                        lhsT=cw[:, lo : lo + P].bitcast(FP8X4),
-                        lhsT_scale=sw[:, lo : lo + P],
-                        rhs=cx[:, c * D : (c + 1) * D].bitcast(FP8X4),
-                        rhs_scale=sx[:, c * D : (c + 1) * D],
-                        start=(c == 0),
-                        stop=(c == PASSES - 1),
-                    )
+                group(ps[:, m * D : (m + 1) * D], cw, sw, D, m * P, b)
+            pss[b] = ps
+
+        def finish(b):
             o_b = outp.tile([P, 2 * D], F32, name="o_b")
-            nc.scalar.copy(out=o_b[:], in_=ps[:])
+            nc.scalar.copy(out=o_b[:], in_=pss[b][:])
             nc.sync.dma_start(
                 out=o_view[:, b], in_=o_b[:].rearrange("p (m e) -> p m e", m=2)
             )
+
+        sum_squares(0)
+        norm(0)
+        sum_squares(1)
+        norm(1)
+        vector_regroup_x(0)
+        vector_regroup_x(1)
+        quantise_x(0)
+
+        for b in range(B - 2):
+            sum_squares(b + 2)
+            if SHARE and b + 3 < B:
+                scalar_regroup_x(b + 3)
+            norm(b + 2)
+            if b >= 1:
+                finish(b - 1)
+            scale(b)
+            quantise_x(b + 1)
+            gw = grp.tile([P, PASSES, D, PACK], BF16, name="gw", align_bytes=64)
+            regroup_both(gw[:], xws[b][:])
+            vector_regroup_x(b + 2)
+            cw, sw = quantise(gw, PASSES * D * PACK, "w", codes)
+            multiply(b, cw, sw)
+
+        y = B - 2
+        z = B - 1
+        scale(y)
+        gw = grp.tile([P, PASSES, D, PACK], BF16, name="gw", align_bytes=64)
+        regroup_pass(nc.scalar.copy, gw[:, 1, :, :], xws[y][:, PACK:, :])
+        quantise_x(z)
+        scale(z)
+        halves = []
+        for m in range(2):
+            gh = keep.tile([P, PASSES, P, PACK], BF16, name="gh%d" % m, align_bytes=64)
+            halves.append(gh)
+        for c in range(PASSES):
+            regroup_pass(
+                nc.scalar.copy,
+                halves[1][:, c, :, :],
+                xws[z][:, c * PACK : (c + 1) * PACK, P:],
+            )
+        finish(y - 1)
+        regroup_pass(nc.vector.tensor_copy, gw[:, 0, :, :], xws[y][:, :PACK, :])
+        cw, sw = quantise(gw, PASSES * D * PACK, "w", codes)
+        multiply(y, cw, sw)
+        regroup_both(halves[0][:], xws[z][:, :, :P])
+        accs = []
+        for m in range(2):
+            ch, sh = quantise(halves[m], PASSES * P * PACK, "h%d" % m, keep)
+            acc = psum1.tile([P, D], F32, name="acc%d" % m)
+            group(acc[:], ch, sh, P, 0, z)
+            accs.append(acc)
+        finish(y)
+        for m in range(2):
+            o_h = keep.tile([P, D], F32, name="o_h%d" % m)
+            if m == 0:
+                nc.vector.tensor_copy(out=o_h[:], in_=accs[m][:])
+            else:
+                nc.scalar.copy(out=o_h[:], in_=accs[m][:])
+            nc.sync.dma_start(out=o_view[:, z, m, :], in_=o_h[:])

@@ -20,7 +20,7 @@ PACK = 4
 PASSES = L // (P * PACK)
 SLOTS = PASSES * PACK
 EPS = 1e-05
-SHARE = 104
+SHARE = 152
 
 
 def tile_globalmixture_t_kernel(tc, inputs, out):

@@ -19,8 +19,10 @@ D = 256
 PACK = 4
 PASSES = L // (P * PACK)
 SLOTS = PASSES * PACK
+WORDS = PASSES * D
 EPS = 1e-05
 SHARE = 152
+FIRST_SHARED = 3
 
 
 def tile_globalmixture_t_kernel(tc, inputs, out):
@@ -58,8 +60,8 @@ def tile_globalmixture_t_kernel(tc, inputs, out):
 
         sums = {}
         norms = {}
-        gxs = {}
-        cxs = {}
+        pairs = {}
+        quantised = {}
         xws = {}
         pss = {}
 
@@ -92,50 +94,42 @@ def tile_globalmixture_t_kernel(tc, inputs, out):
                 in_=src.rearrange("p (g t) (c i) -> p g c t i", t=PACK, i=4),
             )
 
-        def new_gx(b):
-            gx = grp.tile([P, PASSES, D, PACK], BF16, name="gx", align_bytes=64)
-            gxs[b] = gx
+        def pair(b):
+            if b not in pairs:
+                pairs[b] = grp.tile(
+                    [P, 2, PASSES, D, PACK], BF16, name="pair", align_bytes=64
+                )
+            return pairs[b]
+
+        def shared(b):
+            return SHARE // 2 if b >= FIRST_SHARED else 0
 
         def scalar_regroup_x(b):
-            new_gx(b)
-            regroup_pass(
-                nc.scalar.copy,
-                gxs[b][:, 1, D - SHARE :, :],
-                xs[b][:, PACK:, D - SHARE :],
-            )
+            lo = D - shared(b)
+            for c in range(PASSES):
+                regroup_pass(
+                    nc.scalar.copy,
+                    pair(b - 1)[:, 1, c, lo:, :],
+                    xs[b][:, c * PACK : (c + 1) * PACK, lo:],
+                )
 
         def vector_regroup_x(b):
-            if b in gxs:
-                regroup_pass(nc.vector.tensor_copy, gxs[b][:, 0, :, :], xs[b][:, :PACK, :])
-                regroup_pass(
-                    nc.vector.tensor_copy,
-                    gxs[b][:, 1, : D - SHARE, :],
-                    xs[b][:, PACK:, : D - SHARE],
-                )
-            else:
-                new_gx(b)
-                if b == 0:
-                    for c in range(PASSES):
-                        regroup_pass(
-                            nc.vector.tensor_copy,
-                            gxs[b][:, c, :, :],
-                            xs[b][:, c * PACK : (c + 1) * PACK, :],
-                        )
-                else:
-                    regroup_both(gxs[b][:], xs[b][:])
+            lo = D - shared(b)
+            regroup_both(pair(b - 1)[:, 1, :, :lo, :], xs[b][:, :, :lo])
 
-        def quantise(g, width, tag, pool):
+        def quantise(flat, width, tag, pool):
             c = pool.tile([P, width // PACK], U32, name="c" + tag, align_bytes=64)
             s = pool.tile([P, width // PACK], U8, name="s" + tag, align_bytes=64)
-            nc.vector.quantize_mx(
-                out=c[:].bitcast(FP8X4),
-                scales=s[:],
-                in_=g[:].rearrange("p g d t -> p (g d t)"),
-            )
+            nc.vector.quantize_mx(out=c[:].bitcast(FP8X4), scales=s[:], in_=flat)
             return c, s
 
-        def quantise_x(b):
-            cxs[b] = quantise(gxs[b], PASSES * D * PACK, "x", codes)
+        def quantise_pair(b):
+            quantised[b] = quantise(
+                pair(b)[:].rearrange("p h g d t -> p (h g d t)"),
+                2 * WORDS * PACK,
+                "p",
+                codes,
+            )
 
         def scale(b):
             xw = natp.tile([P, SLOTS, D], BF16, name="xw")
@@ -150,19 +144,21 @@ def tile_globalmixture_t_kernel(tc, inputs, out):
             xws[b] = xw
 
         def group(acc, cw, sw, stride, lo, b):
-            cx, sx = cxs[b]
+            cx, sx = quantised[b - 1]
+            base = WORDS if b > 0 else 0
             for c in range(PASSES):
                 nc.tensor.matmul_mx(
                     out=acc,
                     lhsT=cw[:, c * stride + lo : c * stride + lo + P].bitcast(FP8X4),
                     lhsT_scale=sw[:, c * stride + lo : c * stride + lo + P],
-                    rhs=cx[:, c * D : (c + 1) * D].bitcast(FP8X4),
-                    rhs_scale=sx[:, c * D : (c + 1) * D],
+                    rhs=cx[:, base + c * D : base + (c + 1) * D].bitcast(FP8X4),
+                    rhs_scale=sx[:, base + c * D : base + (c + 1) * D],
                     start=(c == 0),
                     stop=(c == PASSES - 1),
                 )
 
-        def multiply(b, cw, sw):
+        def multiply(b):
+            cw, sw = quantised[b]
             ps = psum.tile([P, 2 * D], F32, name="ps")
             for m in range(2):
                 group(ps[:, m * D : (m + 1) * D], cw, sw, D, m * P, b)
@@ -179,31 +175,36 @@ def tile_globalmixture_t_kernel(tc, inputs, out):
         norm(0)
         sum_squares(1)
         norm(1)
-        vector_regroup_x(0)
+        g0 = keep.tile([P, PASSES, D, PACK], BF16, name="g0", align_bytes=64)
+        for c in range(PASSES):
+            regroup_pass(
+                nc.vector.tensor_copy,
+                g0[:, c, :, :],
+                xs[0][:, c * PACK : (c + 1) * PACK, :],
+            )
         vector_regroup_x(1)
-        quantise_x(0)
+        quantised[-1] = quantise(
+            g0[:].rearrange("p g d t -> p (g d t)"), WORDS * PACK, "0", keep
+        )
+        scale(0)
 
         for b in range(B - 2):
             sum_squares(b + 2)
-            if SHARE and b + 3 < B:
+            if b + 3 < B and shared(b + 3):
                 scalar_regroup_x(b + 3)
             norm(b + 2)
             if b >= 1:
                 finish(b - 1)
-            scale(b)
-            quantise_x(b + 1)
-            gw = grp.tile([P, PASSES, D, PACK], BF16, name="gw", align_bytes=64)
-            regroup_both(gw[:], xws[b][:])
+            regroup_both(pair(b)[:, 0], xws[b][:])
             vector_regroup_x(b + 2)
-            cw, sw = quantise(gw, PASSES * D * PACK, "w", codes)
-            multiply(b, cw, sw)
+            scale(b + 1)
+            quantise_pair(b)
+            multiply(b)
 
         y = B - 2
         z = B - 1
-        scale(y)
-        gw = grp.tile([P, PASSES, D, PACK], BF16, name="gw", align_bytes=64)
-        regroup_pass(nc.scalar.copy, gw[:, 1, :, :], xws[y][:, PACK:, :])
-        quantise_x(z)
+        regroup_pass(nc.scalar.copy, pair(y)[:, 0, 1, :, :], xws[y][:, PACK:, :])
+        regroup_pass(nc.vector.tensor_copy, pair(y)[:, 0, 0, :, :], xws[y][:, :PACK, :])
         scale(z)
         halves = []
         for m in range(2):
@@ -216,18 +217,22 @@ def tile_globalmixture_t_kernel(tc, inputs, out):
                 xws[z][:, c * PACK : (c + 1) * PACK, P:],
             )
         finish(y - 1)
-        regroup_pass(nc.vector.tensor_copy, gw[:, 0, :, :], xws[y][:, :PACK, :])
-        cw, sw = quantise(gw, PASSES * D * PACK, "w", codes)
-        multiply(y, cw, sw)
+        quantise_pair(y)
+        multiply(y)
         regroup_both(halves[0][:], xws[z][:, :, :P])
-        accs = []
-        for m in range(2):
-            ch, sh = quantise(halves[m], PASSES * P * PACK, "h%d" % m, keep)
+        accs = {}
+        for m in (1, 0):
+            ch, sh = quantise(
+                halves[m][:].rearrange("p g d t -> p (g d t)"),
+                PASSES * P * PACK,
+                "h%d" % m,
+                keep,
+            )
             acc = psum1.tile([P, D], F32, name="acc%d" % m)
             group(acc[:], ch, sh, P, 0, z)
-            accs.append(acc)
+            accs[m] = acc
         finish(y)
-        for m in range(2):
+        for m in (1, 0):
             o_h = keep.tile([P, D], F32, name="o_h%d" % m)
             if m == 0:
                 nc.vector.tensor_copy(out=o_h[:], in_=accs[m][:])

@@ -1,6 +1,7 @@
 from contextlib import ExitStack
 
 import concourse.mybir as mybir
+from concourse.masks import make_identity
 
 FLOPS = 2 * 16 * 1024 * 256 * 256
 
@@ -21,8 +22,10 @@ PASSES = L // (P * PACK)
 SLOTS = PASSES * PACK
 WORDS = PASSES * D
 EPS = 1e-05
-SHARE = 152
-FIRST_SHARED = 3
+BANK = 512
+POOL_COLS = 176
+SCALAR_COLS = 24
+FIRST_SHARED = 2
 
 
 def tile_globalmixture_t_kernel(tc, inputs, out):
@@ -35,17 +38,19 @@ def tile_globalmixture_t_kernel(tc, inputs, out):
         keep = ctx.enter_context(tc.tile_pool(name="keep", bufs=1))
         junkp = ctx.enter_context(tc.tile_pool(name="junkp", bufs=4))
         small = ctx.enter_context(tc.tile_pool(name="small", bufs=4))
-        natp = ctx.enter_context(tc.tile_pool(name="natp", bufs=2))
         grp = ctx.enter_context(tc.tile_pool(name="grp", bufs=4))
         codes = ctx.enter_context(tc.tile_pool(name="codes", bufs=3))
         outp = ctx.enter_context(tc.tile_pool(name="outp", bufs=4))
         psum = ctx.enter_context(tc.psum_pool(name="psum", bufs=4))
         psum1 = ctx.enter_context(tc.psum_pool(name="psum1", bufs=1))
+        psumw = ctx.enter_context(tc.psum_pool(name="psumw", bufs=2))
 
         eps = keep.tile([P, 1], F32, name="eps")
         nc.vector.memset(eps[:], EPS)
         warm = keep.tile([P, 1], F32, name="warm")
         nc.scalar.activation(out=warm[:], in_=eps[:], func=ACT.Sqrt)
+        ident = keep.tile([P, P], F32, name="ident")
+        make_identity(nc, ident[:])
 
         xs = []
         for b in range(B):
@@ -62,7 +67,7 @@ def tile_globalmixture_t_kernel(tc, inputs, out):
         norms = {}
         pairs = {}
         quantised = {}
-        xws = {}
+        wps = {}
         pss = {}
 
         def sum_squares(b):
@@ -81,6 +86,27 @@ def tile_globalmixture_t_kernel(tc, inputs, out):
             w = small.tile([P, SLOTS], F32, name="w")
             nc.scalar.activation(out=w[:], in_=sums[b][:], func=ACT.Sqrt, bias=eps[:])
             norms[b] = w
+
+        def spread_norm(b):
+            wp = psumw.tile([P, BANK], F32, name="wp")
+            nc.tensor.matmul(
+                wp[:, :SLOTS], lhsT=ident[:], rhs=norms[b][:], start=True, stop=True
+            )
+            wps[b] = wp
+
+        def scale_regroup(b, dst, lo, hi):
+            for c in range(PASSES):
+                w = wps[b][:, c * PACK : (c + 1) * PACK]
+                nc.vector.tensor_tensor(
+                    out=dst[:, c].rearrange("p (c i) t -> p c t i", i=4),
+                    in0=xs[b][:, c * PACK : (c + 1) * PACK, lo:hi].rearrange(
+                        "p t (c i) -> p c t i", i=4
+                    ),
+                    in1=w.unsqueeze(1)
+                    .unsqueeze(3)
+                    .broadcast_to([P, (hi - lo) // 4, PACK, 4]),
+                    op=ALU.mult,
+                )
 
         def regroup_pass(copy, dst, src):
             copy(
@@ -101,11 +127,13 @@ def tile_globalmixture_t_kernel(tc, inputs, out):
                 )
             return pairs[b]
 
-        def shared(b):
-            return SHARE // 2 if b >= FIRST_SHARED else 0
+        def bounds(b):
+            if b < FIRST_SHARED:
+                return D, D
+            return D - SCALAR_COLS - POOL_COLS, D - SCALAR_COLS
 
         def scalar_regroup_x(b):
-            lo = D - shared(b)
+            lo = bounds(b)[1]
             for c in range(PASSES):
                 regroup_pass(
                     nc.scalar.copy,
@@ -113,8 +141,22 @@ def tile_globalmixture_t_kernel(tc, inputs, out):
                     xs[b][:, c * PACK : (c + 1) * PACK, lo:],
                 )
 
+        def pool_copy(out, in_):
+            nc.gpsimd.tensor_scalar(
+                out=out, in0=in_, scalar1=1.0, scalar2=0.0, op0=ALU.mult, op1=ALU.add
+            )
+
+        def pool_regroup_x(b):
+            lo, hi = bounds(b)
+            for c in range(PASSES):
+                regroup_pass(
+                    pool_copy,
+                    pair(b - 1)[:, 1, c, lo:hi, :],
+                    xs[b][:, c * PACK : (c + 1) * PACK, lo:hi],
+                )
+
         def vector_regroup_x(b):
-            lo = D - shared(b)
+            lo = bounds(b)[0]
             regroup_both(pair(b - 1)[:, 1, :, :lo, :], xs[b][:, :, :lo])
 
         def quantise(flat, width, tag, pool):
@@ -130,18 +172,6 @@ def tile_globalmixture_t_kernel(tc, inputs, out):
                 "p",
                 codes,
             )
-
-        def scale(b):
-            xw = natp.tile([P, SLOTS, D], BF16, name="xw")
-            for s in range(SLOTS):
-                nc.vector.tensor_scalar(
-                    out=xw[:, s, :],
-                    in0=xs[b][:, s, :],
-                    scalar1=norms[b][:, s : s + 1],
-                    scalar2=None,
-                    op0=ALU.mult,
-                )
-            xws[b] = xw
 
         def group(acc, cw, sw, stride, lo, b):
             cx, sx = quantised[b - 1]
@@ -173,8 +203,10 @@ def tile_globalmixture_t_kernel(tc, inputs, out):
 
         sum_squares(0)
         norm(0)
+        spread_norm(0)
         sum_squares(1)
         norm(1)
+        spread_norm(1)
         g0 = keep.tile([P, PASSES, D, PACK], BF16, name="g0", align_bytes=64)
         for c in range(PASSES):
             regroup_pass(
@@ -186,40 +218,36 @@ def tile_globalmixture_t_kernel(tc, inputs, out):
         quantised[-1] = quantise(
             g0[:].rearrange("p g d t -> p (g d t)"), WORDS * PACK, "0", keep
         )
-        scale(0)
+        pool_regroup_x(2)
+        scale_regroup(0, pair(0)[:, 0], 0, D)
 
         for b in range(B - 2):
             sum_squares(b + 2)
-            if b + 3 < B and shared(b + 3):
+            if b == 0:
+                scalar_regroup_x(2)
+            if b + 3 < B:
                 scalar_regroup_x(b + 3)
+                pool_regroup_x(b + 3)
             norm(b + 2)
+            spread_norm(b + 2)
             if b >= 1:
                 finish(b - 1)
-            regroup_both(pair(b)[:, 0], xws[b][:])
+            scale_regroup(b + 1, pair(b + 1)[:, 0], 0, D)
             vector_regroup_x(b + 2)
-            scale(b + 1)
             quantise_pair(b)
             multiply(b)
 
         y = B - 2
         z = B - 1
-        regroup_pass(nc.scalar.copy, pair(y)[:, 0, 1, :, :], xws[y][:, PACK:, :])
-        regroup_pass(nc.vector.tensor_copy, pair(y)[:, 0, 0, :, :], xws[y][:, :PACK, :])
-        scale(z)
         halves = []
         for m in range(2):
             gh = keep.tile([P, PASSES, P, PACK], BF16, name="gh%d" % m, align_bytes=64)
             halves.append(gh)
-        for c in range(PASSES):
-            regroup_pass(
-                nc.scalar.copy,
-                halves[1][:, c, :, :],
-                xws[z][:, c * PACK : (c + 1) * PACK, P:],
-            )
+        scale_regroup(z, halves[1], P, D)
         finish(y - 1)
         quantise_pair(y)
         multiply(y)
-        regroup_both(halves[0][:], xws[z][:, :, :P])
+        scale_regroup(z, halves[0], 0, P)
         accs = {}
         for m in (1, 0):
             ch, sh = quantise(

@@ -23,8 +23,8 @@ SLOTS = PASSES * PACK
 WORDS = PASSES * D
 EPS = 1e-05
 BANK = 512
-POOL_COLS = 176
-SCALAR_COLS = 24
+POOL_COLS = 152
+SCALAR_COLS = 48
 FIRST_SHARED = 2
 
 
@@ -57,8 +57,12 @@ def tile_globalmixture_t_kernel(tc, inputs, out):
             x_b = keep.tile([P, SLOTS, D], BF16, name="x%d" % b)
             x_rows = x_b[:].rearrange("p (c t) d -> p c (t d)", c=PASSES)
             if b == 0:
-                for c in range(PASSES):
-                    nc.sync.dma_start(out=x_rows[:, c, :], in_=x_view[:, b, c, :])
+                for lo, hi in ((0, 2), (2, 4)):
+                    nc.sync.dma_start(
+                        out=x_rows[:, 0, lo * D : hi * D],
+                        in_=x_view[:, b, 0, lo * D : hi * D],
+                    )
+                nc.sync.dma_start(out=x_rows[:, 1, :], in_=x_view[:, b, 1, :])
             else:
                 nc.sync.dma_start(out=x_rows, in_=x_view[:, b])
             xs.append(x_b)
@@ -94,8 +98,8 @@ def tile_globalmixture_t_kernel(tc, inputs, out):
             )
             wps[b] = wp
 
-        def scale_regroup(b, dst, lo, hi):
-            for c in range(PASSES):
+        def scale_regroup(b, dst, lo, hi, passes=range(PASSES)):
+            for c in passes:
                 w = wps[b][:, c * PACK : (c + 1) * PACK]
                 nc.vector.tensor_tensor(
                     out=dst[:, c].rearrange("p (c i) t -> p c t i", i=4),
@@ -243,11 +247,21 @@ def tile_globalmixture_t_kernel(tc, inputs, out):
         for m in range(2):
             gh = keep.tile([P, PASSES, P, PACK], BF16, name="gh%d" % m, align_bytes=64)
             halves.append(gh)
-        scale_regroup(z, halves[1], P, D)
+        xz = keep.tile([P, PACK, D], BF16, name="xz")
+        for t in range(PACK):
+            nc.scalar.activation(
+                out=xz[:, t, :],
+                in_=xs[z][:, PACK + t, :],
+                func=ACT.Copy,
+                scale=norms[z][:, PACK + t : PACK + t + 1],
+            )
+        scale_regroup(z, halves[1], P, D, (0,))
+        regroup_pass(nc.scalar.copy, halves[1][:, 1], xz[:, :, P:])
         finish(y - 1)
+        regroup_pass(nc.scalar.copy, halves[0][:, 1], xz[:, :, :P])
         quantise_pair(y)
         multiply(y)
-        scale_regroup(z, halves[0], 0, P)
+        scale_regroup(z, halves[0], 0, P, (0,))
         accs = {}
         for m in (1, 0):
             ch, sh = quantise(

@@ -23,7 +23,7 @@ SLOTS = PASSES * PACK
 WORDS = PASSES * D
 EPS = 1e-05
 BANK = 512
-POOL_COLS = 152
+POOL_COLS = 180
 SCALAR_COLS = 48
 FIRST_SHARED = 2
 
@@ -74,9 +74,11 @@ def tile_globalmixture_t_kernel(tc, inputs, out):
         wps = {}
         pss = {}
 
-        def sum_squares(b):
-            ss = small.tile([P, SLOTS], F32, name="ss")
-            for s in range(SLOTS):
+        def sum_squares(b, slots=range(SLOTS)):
+            if b not in sums:
+                sums[b] = small.tile([P, SLOTS], F32, name="ss")
+            ss = sums[b]
+            for s in slots:
                 junk = junkp.tile([P, D], BF16, name="junk")
                 nc.scalar.activation(
                     out=junk[:],
@@ -84,7 +86,6 @@ def tile_globalmixture_t_kernel(tc, inputs, out):
                     func=ACT.Square,
                     accum_out=ss[:, s : s + 1],
                 )
-            sums[b] = ss
 
         def norm(b):
             w = small.tile([P, SLOTS], F32, name="w")
@@ -206,9 +207,11 @@ def tile_globalmixture_t_kernel(tc, inputs, out):
             )
 
         sum_squares(0)
+        sum_squares(1, range(1))
         norm(0)
         spread_norm(0)
-        sum_squares(1)
+        sum_squares(1, range(1, SLOTS))
+        sum_squares(2, range(1))
         norm(1)
         spread_norm(1)
         g0 = keep.tile([P, PASSES, D, PACK], BF16, name="g0", align_bytes=64)
@@ -218,15 +221,15 @@ def tile_globalmixture_t_kernel(tc, inputs, out):
                 g0[:, c, :, :],
                 xs[0][:, c * PACK : (c + 1) * PACK, :],
             )
-        vector_regroup_x(1)
         quantised[-1] = quantise(
             g0[:].rearrange("p g d t -> p (g d t)"), WORDS * PACK, "0", keep
         )
+        vector_regroup_x(1)
         pool_regroup_x(2)
         scale_regroup(0, pair(0)[:, 0], 0, D)
 
         for b in range(B - 2):
-            sum_squares(b + 2)
+            sum_squares(b + 2, range(1 if b == 0 else 0, SLOTS))
             if b == 0:
                 scalar_regroup_x(2)
             if b + 3 < B:

@@ -23,8 +23,8 @@ SLOTS = PASSES * PACK
 WORDS = PASSES * D
 EPS = 1e-05
 BANK = 512
-POOL_COLS = 180
-SCALAR_COLS = 48
+POOL_COLS = 176
+SCALAR_COLS = 56
 FIRST_SHARED = 2
 
 
@@ -113,10 +113,10 @@ def tile_globalmixture_t_kernel(tc, inputs, out):
                     op=ALU.mult,
                 )
 
-        def regroup_pass(copy, dst, src):
+        def regroup_pass(copy, dst, src, run=4):
             copy(
-                out=dst.rearrange("p (c i) t -> p c t i", i=4),
-                in_=src.rearrange("p t (c i) -> p c t i", i=4),
+                out=dst.rearrange("p (c i) t -> p c t i", i=run),
+                in_=src.rearrange("p t (c i) -> p c t i", i=run),
             )
 
         def regroup_both(dst, src):
@@ -158,6 +158,7 @@ def tile_globalmixture_t_kernel(tc, inputs, out):
                     pool_copy,
                     pair(b - 1)[:, 1, c, lo:hi, :],
                     xs[b][:, c * PACK : (c + 1) * PACK, lo:hi],
+                    8,
                 )
 
         def vector_regroup_x(b):

from contextlib import ExitStack

import concourse.mybir as mybir
from concourse.masks import make_identity

FLOPS = 2 * 16 * 1024 * 256 * 256

BF16 = mybir.dt.bfloat16
F32 = mybir.dt.float32
U32 = mybir.dt.uint32
U8 = mybir.dt.uint8
FP8X4 = mybir.dt.float8_e4m3fn_x4
ACT = mybir.ActivationFunctionType
ALU = mybir.AluOpType

P = 128
B = 16
L = 1024
D = 256
PACK = 4
PASSES = L // (P * PACK)
SLOTS = PASSES * PACK
WORDS = PASSES * D
EPS = 1e-05
BANK = 512
POOL_COLS = 176
SCALAR_COLS = 56
FIRST_SHARED = 2


def tile_globalmixture_t_kernel(tc, inputs, out):
    nc = tc.nc
    x_view = inputs.rearrange("b (c p t) d -> p b c (t d)", c=PASSES, p=P, t=PACK)
    o_view = out.rearrange("b (m p) e -> p b m e", m=2, p=P)

    with ExitStack() as ctx:
        ctx.enter_context(tc.manual_schedule())
        keep = ctx.enter_context(tc.tile_pool(name="keep", bufs=1))
        junkp = ctx.enter_context(tc.tile_pool(name="junkp", bufs=4))
        small = ctx.enter_context(tc.tile_pool(name="small", bufs=4))
        grp = ctx.enter_context(tc.tile_pool(name="grp", bufs=4))
        codes = ctx.enter_context(tc.tile_pool(name="codes", bufs=3))
        outp = ctx.enter_context(tc.tile_pool(name="outp", bufs=4))
        psum = ctx.enter_context(tc.psum_pool(name="psum", bufs=4))
        psum1 = ctx.enter_context(tc.psum_pool(name="psum1", bufs=1))
        psumw = ctx.enter_context(tc.psum_pool(name="psumw", bufs=2))

        eps = keep.tile([P, 1], F32, name="eps")
        nc.vector.memset(eps[:], EPS)
        warm = keep.tile([P, 1], F32, name="warm")
        nc.scalar.activation(out=warm[:], in_=eps[:], func=ACT.Sqrt)
        ident = keep.tile([P, P], F32, name="ident")
        make_identity(nc, ident[:])

        xs = []
        for b in range(B):
            x_b = keep.tile([P, SLOTS, D], BF16, name="x%d" % b)
            x_rows = x_b[:].rearrange("p (c t) d -> p c (t d)", c=PASSES)
            if b == 0:
                for lo, hi in ((0, 2), (2, 4)):
                    nc.sync.dma_start(
                        out=x_rows[:, 0, lo * D : hi * D],
                        in_=x_view[:, b, 0, lo * D : hi * D],
                    )
                nc.sync.dma_start(out=x_rows[:, 1, :], in_=x_view[:, b, 1, :])
            else:
                nc.sync.dma_start(out=x_rows, in_=x_view[:, b])
            xs.append(x_b)

        sums = {}
        norms = {}
        pairs = {}
        quantised = {}
        wps = {}
        pss = {}

        def sum_squares(b, slots=range(SLOTS)):
            if b not in sums:
                sums[b] = small.tile([P, SLOTS], F32, name="ss")
            ss = sums[b]
            for s in slots:
                junk = junkp.tile([P, D], BF16, name="junk")
                nc.scalar.activation(
                    out=junk[:],
                    in_=xs[b][:, s, :],
                    func=ACT.Square,
                    accum_out=ss[:, s : s + 1],
                )

        def norm(b):
            w = small.tile([P, SLOTS], F32, name="w")
            nc.scalar.activation(out=w[:], in_=sums[b][:], func=ACT.Sqrt, bias=eps[:])
            norms[b] = w

        def spread_norm(b):
            wp = psumw.tile([P, BANK], F32, name="wp")
            nc.tensor.matmul(
                wp[:, :SLOTS], lhsT=ident[:], rhs=norms[b][:], start=True, stop=True
            )
            wps[b] = wp

        def scale_regroup(b, dst, lo, hi, passes=range(PASSES)):
            for c in passes:
                w = wps[b][:, c * PACK : (c + 1) * PACK]
                nc.vector.tensor_tensor(
                    out=dst[:, c].rearrange("p (c i) t -> p c t i", i=4),
                    in0=xs[b][:, c * PACK : (c + 1) * PACK, lo:hi].rearrange(
                        "p t (c i) -> p c t i", i=4
                    ),
                    in1=w.unsqueeze(1)
                    .unsqueeze(3)
                    .broadcast_to([P, (hi - lo) // 4, PACK, 4]),
                    op=ALU.mult,
                )

        def regroup_pass(copy, dst, src, run=4):
            copy(
                out=dst.rearrange("p (c i) t -> p c t i", i=run),
                in_=src.rearrange("p t (c i) -> p c t i", i=run),
            )

        def regroup_both(dst, src):
            nc.vector.tensor_copy(
                out=dst.rearrange("p g (c i) t -> p g c t i", i=4),
                in_=src.rearrange("p (g t) (c i) -> p g c t i", t=PACK, i=4),
            )

        def pair(b):
            if b not in pairs:
                pairs[b] = grp.tile(
                    [P, 2, PASSES, D, PACK], BF16, name="pair", align_bytes=64
                )
            return pairs[b]

        def bounds(b):
            if b < FIRST_SHARED:
                return D, D
            return D - SCALAR_COLS - POOL_COLS, D - SCALAR_COLS

        def scalar_regroup_x(b):
            lo = bounds(b)[1]
            for c in range(PASSES):
                regroup_pass(
                    nc.scalar.copy,
                    pair(b - 1)[:, 1, c, lo:, :],
                    xs[b][:, c * PACK : (c + 1) * PACK, lo:],
                )

        def pool_copy(out, in_):
            nc.gpsimd.tensor_scalar(
                out=out, in0=in_, scalar1=1.0, scalar2=0.0, op0=ALU.mult, op1=ALU.add
            )

        def pool_regroup_x(b):
            lo, hi = bounds(b)
            for c in range(PASSES):
                regroup_pass(
                    pool_copy,
                    pair(b - 1)[:, 1, c, lo:hi, :],
                    xs[b][:, c * PACK : (c + 1) * PACK, lo:hi],
                    8,
                )

        def vector_regroup_x(b):
            lo = bounds(b)[0]
            regroup_both(pair(b - 1)[:, 1, :, :lo, :], xs[b][:, :, :lo])

        def quantise(flat, width, tag, pool):
            c = pool.tile([P, width // PACK], U32, name="c" + tag, align_bytes=64)
            s = pool.tile([P, width // PACK], U8, name="s" + tag, align_bytes=64)
            nc.vector.quantize_mx(out=c[:].bitcast(FP8X4), scales=s[:], in_=flat)
            return c, s

        def quantise_pair(b):
            quantised[b] = quantise(
                pair(b)[:].rearrange("p h g d t -> p (h g d t)"),
                2 * WORDS * PACK,
                "p",
                codes,
            )

        def group(acc, cw, sw, stride, lo, b):
            cx, sx = quantised[b - 1]
            base = WORDS if b > 0 else 0
            for c in range(PASSES):
                nc.tensor.matmul_mx(
                    out=acc,
                    lhsT=cw[:, c * stride + lo : c * stride + lo + P].bitcast(FP8X4),
                    lhsT_scale=sw[:, c * stride + lo : c * stride + lo + P],
                    rhs=cx[:, base + c * D : base + (c + 1) * D].bitcast(FP8X4),
                    rhs_scale=sx[:, base + c * D : base + (c + 1) * D],
                    start=(c == 0),
                    stop=(c == PASSES - 1),
                )

        def multiply(b):
            cw, sw = quantised[b]
            ps = psum.tile([P, 2 * D], F32, name="ps")
            for m in range(2):
                group(ps[:, m * D : (m + 1) * D], cw, sw, D, m * P, b)
            pss[b] = ps

        def finish(b):
            o_b = outp.tile([P, 2 * D], F32, name="o_b")
            nc.scalar.copy(out=o_b[:], in_=pss[b][:])
            nc.sync.dma_start(
                out=o_view[:, b], in_=o_b[:].rearrange("p (m e) -> p m e", m=2)
            )

        sum_squares(0)
        sum_squares(1, range(1))
        norm(0)
        spread_norm(0)
        sum_squares(1, range(1, SLOTS))
        sum_squares(2, range(1))
        norm(1)
        spread_norm(1)
        g0 = keep.tile([P, PASSES, D, PACK], BF16, name="g0", align_bytes=64)
        for c in range(PASSES):
            regroup_pass(
                nc.vector.tensor_copy,
                g0[:, c, :, :],
                xs[0][:, c * PACK : (c + 1) * PACK, :],
            )
        quantised[-1] = quantise(
            g0[:].rearrange("p g d t -> p (g d t)"), WORDS * PACK, "0", keep
        )
        vector_regroup_x(1)
        pool_regroup_x(2)
        scale_regroup(0, pair(0)[:, 0], 0, D)

        for b in range(B - 2):
            sum_squares(b + 2, range(1 if b == 0 else 0, SLOTS))
            if b == 0:
                scalar_regroup_x(2)
            if b + 3 < B:
                scalar_regroup_x(b + 3)
                pool_regroup_x(b + 3)
            norm(b + 2)
            spread_norm(b + 2)
            if b >= 1:
                finish(b - 1)
            scale_regroup(b + 1, pair(b + 1)[:, 0], 0, D)
            vector_regroup_x(b + 2)
            quantise_pair(b)
            multiply(b)

        y = B - 2
        z = B - 1
        halves = []
        for m in range(2):
            gh = keep.tile([P, PASSES, P, PACK], BF16, name="gh%d" % m, align_bytes=64)
            halves.append(gh)
        xz = keep.tile([P, PACK, D], BF16, name="xz")
        for t in range(PACK):
            nc.scalar.activation(
                out=xz[:, t, :],
                in_=xs[z][:, PACK + t, :],
                func=ACT.Copy,
                scale=norms[z][:, PACK + t : PACK + t + 1],
            )
        scale_regroup(z, halves[1], P, D, (0,))
        regroup_pass(nc.scalar.copy, halves[1][:, 1], xz[:, :, P:])
        finish(y - 1)
        regroup_pass(nc.scalar.copy, halves[0][:, 1], xz[:, :, :P])
        quantise_pair(y)
        multiply(y)
        scale_regroup(z, halves[0], 0, P, (0,))
        accs = {}
        for m in (1, 0):
            ch, sh = quantise(
                halves[m][:].rearrange("p g d t -> p (g d t)"),
                PASSES * P * PACK,
                "h%d" % m,
                keep,
            )
            acc = psum1.tile([P, D], F32, name="acc%d" % m)
            group(acc[:], ch, sh, P, 0, z)
            accs[m] = acc
        finish(y)
        for m in (1, 0):
            o_h = keep.tile([P, D], F32, name="o_h%d" % m)
            if m == 0:
                nc.vector.tensor_copy(out=o_h[:], in_=accs[m][:])
            else:
                nc.scalar.copy(out=o_h[:], in_=accs[m][:])
            nc.sync.dma_start(out=o_view[:, z, m, :], in_=o_h[:])
